import numpy as np
import ml_dtypes


def mxq(x, axis, fmt="e4m3"):
    dtype, down = {"e4m3": (ml_dtypes.float8_e4m3fn, 7), "e5m2": (ml_dtypes.float8_e5m2, 14)}[fmt]
    v = np.moveaxis(np.asarray(x, np.float32).astype(ml_dtypes.bfloat16).astype(np.float64), axis, -1)
    blocks = v.reshape(v.shape[:-1] + (-1, 32))
    amax = np.abs(blocks).max(-1, keepdims=True)
    byte = np.maximum(np.where(amax > 0, np.frexp(amax)[1] - 1 + 127, 0) - down, 1)
    scale = np.exp2(byte - 127.0)
    codes = (blocks / scale).astype(np.float32).astype(dtype).astype(np.float64)
    return np.moveaxis((codes * scale).reshape(v.shape), -1, axis)


WIDE = False


def mx_kscale(k):
    if not WIDE:
        return np.ones(k)
    levels = np.array([10, -10, 5, -5, 0])
    if k % 512:
        return np.exp2(np.random.permutation(np.resize(levels, k // 32))).repeat(32)
    a = np.empty((k // 512, 16))
    for p in range(k // 512):
        a[p, :8] = np.random.permutation(np.resize(levels, 8))
        for g in range(8):
            far = levels[np.abs(levels - a[p, g]) >= 10]
            a[p, g + 8] = far[np.random.randint(len(far))]
    return np.exp2(a.ravel()).repeat(32)


BF16 = ml_dtypes.bfloat16


def bf(x):
    return np.asarray(x, np.float32).astype(BF16)


def f64(x):
    return np.asarray(x).astype(np.float64)


B, H, L, E, QD = 8, 1, 128, 2048, 512
T = B * H * L


def setup_inputs():
    s = mx_kscale(T).reshape(B, H, L, 1)
    u = mx_kscale(QD)
    x0 = bf(np.random.standard_normal((B, H, L, E)))
    Wk0 = bf(np.random.standard_normal((QD, E)) * 0.3 / np.sqrt(E))
    bk = bf(0.1 + 0.1 * np.random.standard_normal(QD))
    Wv0 = bf(np.random.standard_normal((QD, E)) * 0.3 / np.sqrt(E))
    bv = bf(0.1 + 0.1 * np.random.standard_normal(QD))
    g = bf(np.random.standard_normal((B, H, L, QD)) * np.exp2(np.random.randint(-6, 1, (B, H, L, 1))) * 16.0 / s * u)
    K = f64(x0) @ f64(Wk0).T + f64(bk)
    V = f64(x0) @ f64(Wv0).T + f64(bv)
    return {"x": bf(f64(x0) * s),
            "Wk": bf(f64(Wk0) / u[:, None]),
            "bk": bk,
            "Wv": bf(f64(Wv0) / u[:, None]),
            "bv": bv,
            "K": np.asarray(K, np.float32),
            "V": np.asarray(V, np.float32),
            "grad_out": g}


def reference(x, Wk, bk, Wv, bv, K, V, grad_out):
    g = f64(grad_out).reshape(T, QD)
    dK = g * f64(V).reshape(T, QD)
    dV = g * f64(K).reshape(T, QD)
    a = mxq(dK, 1, "e5m2") @ mxq(f64(Wk), 0, "e4m3")
    c = mxq(dV, 1, "e5m2") @ mxq(f64(Wv), 0, "e4m3")
    dx = (a + c).reshape(B, H, L, E)
    dWk = mxq(dK, 0, "e5m2").T @ mxq(f64(x).reshape(T, E), 0, "e4m3")
    return dx, dWk

@@ -1,0 +1,180 @@
+from contextlib import ExitStack
+
+import concourse.mybir as mybir
+from concourse.masks import make_identity
+
+F32 = mybir.dt.float32
+BF16 = mybir.dt.bfloat16
+U32 = mybir.dt.uint32
+U8 = mybir.dt.uint8
+E4M3 = mybir.dt.float8_e4m3fn_x4
+E5M2 = mybir.dt.float8_e5m2_x4
+MULT = mybir.AluOpType.mult
+
+P = 128
+PACK = 4
+T, QD, E = 1024, 512, 2048
+K_PASS = P * PACK
+G = T // K_PASS
+N_TILE = 512
+NCH = E // N_TILE
+NMB = QD // P
+WIDE = PACK * N_TILE
+
+FLOPS = 2 * T * QD * E * 3
+BYTES = 2 * (T * E + 2 * QD * E + T * QD) + 4 * (2 * T * QD) + 4 * (T * E + QD * E)
+
+
+def tile_parallelretention_pa_v_kernel(tc, x, Wk, bk, Wv, bv, K, V, grad_out, out_0, out_1):
+    nc = tc.nc
+
+    x_v = x.flatten_outer_dims().rearrange("(g p j) e -> g p j e", g=G, j=PACK)
+    go_v = grad_out.flatten_outer_dims().rearrange("(g p j) w -> g p (j w)", g=G, j=PACK)
+    k_v = K.flatten_outer_dims().rearrange("(g p j) w -> g p (j w)", g=G, j=PACK)
+    v_v = V.flatten_outer_dims().rearrange("(g p j) w -> g p (j w)", g=G, j=PACK)
+    wk_v = Wk.rearrange("(p j) e -> p j e", j=PACK)
+    wv_v = Wv.rearrange("(p j) e -> p j e", j=PACK)
+    o0_v = out_0.flatten_outer_dims().rearrange("(g p j) e -> g j p e", g=G, j=PACK)
+    o1_v = out_1.rearrange("(m p) e -> m p e", p=P)
+
+    with ExitStack() as ctx:
+        keep = ctx.enter_context(tc.tile_pool(name="keep", bufs=1))
+        slabs = ctx.enter_context(tc.tile_pool(name="slabs", bufs=8))
+        grps = ctx.enter_context(tc.tile_pool(name="grps", bufs=5))
+        ps_t = ctx.enter_context(tc.psum_pool(name="ps_t", bufs=2))
+        ps_a = ctx.enter_context(tc.psum_pool(name="ps_a", bufs=6))
+
+        go_r, v_r, k_r, x_r = [], [], [], []
+
+        def load_dz_inputs(g):
+            go = keep.tile([P, WIDE], BF16, name="go%d" % g)
+            nc.sync.dma_start(out=go[:], in_=go_v[g])
+            vv = slabs.tile([P, WIDE], F32, name="v%d" % g, tag="slab")
+            nc.sync.dma_start(out=vv[:], in_=v_v[g])
+            kk = slabs.tile([P, WIDE], F32, name="k%d" % g, tag="slab")
+            nc.sync.dma_start(out=kk[:], in_=k_v[g])
+            go_r.append(go)
+            v_r.append(vv)
+            k_r.append(kk)
+
+        load_dz_inputs(0)
+        wk_r = keep.tile([P, PACK, E], BF16, name="wk_r")
+        nc.sync.dma_start(out=wk_r[:], in_=wk_v)
+        wv_r = keep.tile([P, PACK, E], BF16, name="wv_r")
+        nc.sync.dma_start(out=wv_r[:], in_=wv_v)
+        load_dz_inputs(1)
+        for g in range(G):
+            xr = keep.tile([P, PACK, E], BF16, name="x_r%d" % g)
+            nc.sync.dma_start(out=xr[:], in_=x_v[g])
+            x_r.append(xr)
+
+        ident = keep.tile([P, P], F32, name="ident")
+        make_identity(nc, ident[:])
+        warm = keep.tile([P, 8], F32, name="warm")
+        nc.vector.memset(warm[:], 0.0)
+        warm2 = keep.tile([P, 8], F32, name="warm2")
+        nc.scalar.copy(out=warm2[:], in_=warm[:])
+
+        def copy_on(eng, out, in_):
+            if eng == "V":
+                nc.vector.tensor_copy(out=out, in_=in_)
+            else:
+                nc.scalar.copy(out=out, in_=in_)
+
+        def quantize(grp, fmt, name):
+            codes = keep.tile([P, N_TILE], U32, name=name + "_c", align_bytes=64)
+            scales = keep.tile([P, N_TILE], U8, name=name + "_s", align_bytes=64)
+            nc.vector.quantize_mx(out=codes[:].bitcast(fmt), scales=scales[:], in_=grp[:])
+            return codes, scales
+
+        def interleave(eng, src_pjw):
+            grp = grps.tile([P, WIDE], BF16, name="grp", tag="grp", align_bytes=64)
+            copy_on(eng, grp[:].rearrange("p (w j) -> p w j", j=PACK), src_pjw.rearrange("p j w -> p w j"))
+            return grp
+
+        dkt, dvt, dki = [], [], []
+
+        def transposed(dz):
+            words = dz[:].bitcast(F32)
+            grp = grps.tile([P, WIDE], BF16, name="grp", tag="grp", align_bytes=64)
+            grp_w = grp[:].bitcast(F32).rearrange("q (j p u) -> q j p u", j=PACK, u=2)
+            for b in range(2):
+                tp = ps_t.tile([P, 4, P], F32, name="tp", tag="tp")
+                for jj in range(2):
+                    j = 2 * b + jj
+                    for u in range(2):
+                        nc.tensor.transpose(tp[:, 2 * jj + u, :], words[:, 256 * j + u : 256 * (j + 1) : 2], ident[:])
+                nc.scalar.copy(out=grp_w[:, 2 * b : 2 * b + 2, :, :], in_=tp[:].rearrange("q (j u) p -> q j p u", u=2))
+            return grp
+
+        def stage_g(g):
+            dk = keep.tile([P, WIDE], BF16, name="dk%d" % g)
+            nc.vector.tensor_tensor(out=dk[:], in0=go_r[g][:], in1=v_r[g][:], op=MULT)
+            dv = keep.tile([P, WIDE], BF16, name="dv%d" % g)
+            nc.vector.tensor_tensor(out=dv[:], in0=go_r[g][:], in1=k_r[g][:], op=MULT)
+            gk = transposed(dk)
+            gv = transposed(dv)
+            dkt.append(quantize(gk, E5M2, "dkt%d" % g))
+            dvt.append(quantize(gv, E5M2, "dvt%d" % g))
+            gi = interleave("S", dk[:].rearrange("p (j w) -> p j w", j=PACK))
+            dki.append(quantize(gi, E5M2, "dki%d" % g))
+
+        wk_q, wv_q = [], []
+
+        def stage_w(c):
+            eng = "V" if c < 2 else "S"
+            cols = slice(c * N_TILE, (c + 1) * N_TILE)
+            ga = interleave(eng, wk_r[:, :, cols])
+            gb = interleave(eng, wv_r[:, :, cols])
+            wk_q.append(quantize(ga, E4M3, "wk%d" % c))
+            wv_q.append(quantize(gb, E4M3, "wv%d" % c))
+
+        x_q = {}
+
+        def stage_x(g, c):
+            cols = slice(c * N_TILE, (c + 1) * N_TILE)
+            gx = interleave("V", x_r[g][:, :, cols])
+            x_q[(g, c)] = quantize(gx, E4M3, "x%d_%d" % (g, c))
+
+        def mx(acc, a, m, b, start, stop):
+            mc = slice(m * P, (m + 1) * P)
+            nc.tensor.matmul_mx(
+                out=acc[:],
+                lhsT=a[0][:, mc].bitcast(E5M2),
+                lhsT_scale=a[1][:, mc],
+                rhs=b[0][:].bitcast(E4M3),
+                rhs_scale=b[1][:],
+                start=start,
+                stop=stop,
+            )
+
+        def out0_rows(g, j):
+            st = slabs.tile([P, E], F32, name="st", tag="slab")
+            for c in range(NCH):
+                acc = ps_a.tile([P, N_TILE], F32, name="acc", tag="acc")
+                mx(acc, dkt[g], j, wk_q[c], True, False)
+                mx(acc, dvt[g], j, wv_q[c], False, True)
+                copy_on("S", st[:, c * N_TILE : (c + 1) * N_TILE], acc[:])
+            nc.sync.dma_start(out=o0_v[g, j], in_=st[:])
+
+        def out1_rows(m, h):
+            st = slabs.tile([P, E // 2], F32, name="st", tag="slab")
+            for cc in range(2):
+                c = 2 * h + cc
+                acc = ps_a.tile([P, N_TILE], F32, name="acc", tag="acc")
+                mx(acc, dki[0], m, x_q[(0, c)], True, False)
+                mx(acc, dki[1], m, x_q[(1, c)], False, True)
+                copy_on("V" if cc == 1 else "S", st[:, cc * N_TILE : (cc + 1) * N_TILE], acc[:])
+            nc.sync.dma_start(out=o1_v[m][:, h * (E // 2) : (h + 1) * (E // 2)], in_=st[:])
+
+        stage_g(0)
+        for c in range(NCH):
+            stage_w(c)
+        stage_g(1)
+        for g in range(G):
+            for j in range(PACK):
+                out0_rows(g, j)
+                stage_x(j % 2, 2 * g + j // 2)
+        for h in range(2):
+            for m in range(NMB):
+                out1_rows(m, h)

@@ -20,6 +20,8 @@ N_TILE = 512
 NCH = E // N_TILE
 NMB = QD // P
 WIDE = PACK * N_TILE
+HALF = WIDE // 2
+EH = E // 2
 
 FLOPS = 2 * T * QD * E * 3
 BYTES = 2 * (T * E + 2 * QD * E + T * QD) + 4 * (2 * T * QD) + 4 * (T * E + QD * E)
@@ -32,37 +34,41 @@ def tile_parallelretention_pa_v_kernel(tc, x, Wk, bk, Wv, bv, K, V, grad_out, ou
     go_v = grad_out.flatten_outer_dims().rearrange("(g p j) w -> g p (j w)", g=G, j=PACK)
     k_v = K.flatten_outer_dims().rearrange("(g p j) w -> g p (j w)", g=G, j=PACK)
     v_v = V.flatten_outer_dims().rearrange("(g p j) w -> g p (j w)", g=G, j=PACK)
-    wk_v = Wk.rearrange("(p j) e -> p j e", j=PACK)
-    wv_v = Wv.rearrange("(p j) e -> p j e", j=PACK)
+    w_v = {"k": Wk.rearrange("(p j) e -> p j e", j=PACK), "v": Wv.rearrange("(p j) e -> p j e", j=PACK)}
     o0_v = out_0.flatten_outer_dims().rearrange("(g p j) e -> g j p e", g=G, j=PACK)
     o1_v = out_1.rearrange("(m p) e -> m p e", p=P)
 
     with ExitStack() as ctx:
         keep = ctx.enter_context(tc.tile_pool(name="keep", bufs=1))
-        slabs = ctx.enter_context(tc.tile_pool(name="slabs", bufs=8))
-        grps = ctx.enter_context(tc.tile_pool(name="grps", bufs=5))
-        ps_t = ctx.enter_context(tc.psum_pool(name="ps_t", bufs=2))
-        ps_a = ctx.enter_context(tc.psum_pool(name="ps_a", bufs=6))
+        slabs = ctx.enter_context(tc.tile_pool(name="slabs", bufs=9))
+        grps = ctx.enter_context(tc.tile_pool(name="grps", bufs=6))
+        ps_x = ctx.enter_context(tc.psum_pool(name="ps_x", bufs=3))
+        ps_a = ctx.enter_context(tc.psum_pool(name="ps_a", bufs=5))
+        ctx.enter_context(tc.manual_schedule())
 
-        go_r, v_r, k_r, x_r = [], [], [], []
-
-        def load_dz_inputs(g):
-            go = keep.tile([P, WIDE], BF16, name="go%d" % g)
-            nc.sync.dma_start(out=go[:], in_=go_v[g])
-            vv = slabs.tile([P, WIDE], F32, name="v%d" % g, tag="slab")
-            nc.sync.dma_start(out=vv[:], in_=v_v[g])
-            kk = slabs.tile([P, WIDE], F32, name="k%d" % g, tag="slab")
-            nc.sync.dma_start(out=kk[:], in_=k_v[g])
-            go_r.append(go)
-            v_r.append(vv)
-            k_r.append(kk)
-
-        load_dz_inputs(0)
-        wk_r = keep.tile([P, PACK, E], BF16, name="wk_r")
-        nc.sync.dma_start(out=wk_r[:], in_=wk_v)
-        wv_r = keep.tile([P, PACK, E], BF16, name="wv_r")
-        nc.sync.dma_start(out=wv_r[:], in_=wv_v)
-        load_dz_inputs(1)
+        go_r, v_r, k_r = {}, {}, {}
+        for b in range(2):
+            cols = slice(b * HALF, (b + 1) * HALF)
+            go_r[(0, b)] = keep.tile([P, HALF], BF16, name="go0%d" % b)
+            nc.sync.dma_start(out=go_r[(0, b)][:], in_=go_v[0][:, cols])
+            v_r[(0, b)] = keep.tile([P, HALF], F32, name="v0%d" % b)
+            nc.sync.dma_start(out=v_r[(0, b)][:], in_=v_v[0][:, cols])
+        for b in range(2):
+            cols = slice(b * HALF, (b + 1) * HALF)
+            k_r[(0, b)] = keep.tile([P, HALF], F32, name="k0%d" % b)
+            nc.sync.dma_start(out=k_r[(0, b)][:], in_=k_v[0][:, cols])
+        w_r = {}
+        for h in range(2):
+            for w in ("k", "v"):
+                w_r[(w, h)] = slabs.tile([P, PACK, EH], BF16, name="w_r", tag="slab")
+                nc.sync.dma_start(out=w_r[(w, h)][:], in_=w_v[w][:, :, h * EH : (h + 1) * EH])
+        go1 = keep.tile([P, WIDE], BF16, name="go1")
+        nc.sync.dma_start(out=go1[:], in_=go_v[1])
+        v1 = slabs.tile([P, WIDE], F32, name="v1", tag="slab")
+        nc.sync.dma_start(out=v1[:], in_=v_v[1])
+        k1 = slabs.tile([P, WIDE], F32, name="k1", tag="slab")
+        nc.sync.dma_start(out=k1[:], in_=k_v[1])
+        x_r = []
         for g in range(G):
             xr = keep.tile([P, PACK, E], BF16, name="x_r%d" % g)
             nc.sync.dma_start(out=xr[:], in_=x_v[g])
@@ -70,16 +76,16 @@ def tile_parallelretention_pa_v_kernel(tc, x, Wk, bk, Wv, bv, K, V, grad_out, ou
 
         ident = keep.tile([P, P], F32, name="ident")
         make_identity(nc, ident[:])
+        ident_b = keep.tile([P, P], BF16, name="ident_b")
+        make_identity(nc, ident_b[:])
         warm = keep.tile([P, 8], F32, name="warm")
         nc.vector.memset(warm[:], 0.0)
         warm2 = keep.tile([P, 8], F32, name="warm2")
         nc.scalar.copy(out=warm2[:], in_=warm[:])
 
-        def copy_on(eng, out, in_):
-            if eng == "V":
-                nc.vector.tensor_copy(out=out, in_=in_)
-            else:
-                nc.scalar.copy(out=out, in_=in_)
+        def new_grp():
+            grp = grps.tile([P, WIDE], BF16, name="grp", tag="grp", align_bytes=64)
+            return grp
 
         def quantize(grp, fmt, name):
             codes = keep.tile([P, N_TILE], U32, name=name + "_c", align_bytes=64)
@@ -87,54 +93,36 @@ def tile_parallelretention_pa_v_kernel(tc, x, Wk, bk, Wv, bv, K, V, grad_out, ou
             nc.vector.quantize_mx(out=codes[:].bitcast(fmt), scales=scales[:], in_=grp[:])
             return codes, scales
 
-        def interleave(eng, src_pjw):
-            grp = grps.tile([P, WIDE], BF16, name="grp", tag="grp", align_bytes=64)
-            copy_on(eng, grp[:].rearrange("p (w j) -> p w j", j=PACK), src_pjw.rearrange("p j w -> p w j"))
+        def interleave_v(src_pjw):
+            grp = new_grp()
+            nc.vector.tensor_copy(out=grp[:].rearrange("p (w j) -> p w j", j=PACK), in_=src_pjw.rearrange("p j w -> p w j"))
             return grp
 
-        dkt, dvt, dki = [], [], []
+        def interleave_pe(src_pjw):
+            grp = new_grp()
+            for hb in range(2):
+                mv = ps_x.tile([P, 2 * N_TILE], BF16, name="mv", tag="aux")
+                for q in range(2):
+                    c0 = hb * 256 + q * P
+                    nc.tensor.matmul(
+                        out=mv[:, q * N_TILE : (q + 1) * N_TILE],
+                        lhsT=ident_b[:],
+                        rhs=src_pjw[:, :, c0 : c0 + P].rearrange("p j w -> p w j"),
+                        start=True,
+                        stop=True,
+                    )
+                nc.scalar.copy(out=grp[:, hb * HALF : (hb + 1) * HALF], in_=mv[:])
+            return grp
 
-        def transposed(dz):
+        def transpose_half(dz, grp, b):
             words = dz[:].bitcast(F32)
-            grp = grps.tile([P, WIDE], BF16, name="grp", tag="grp", align_bytes=64)
             grp_w = grp[:].bitcast(F32).rearrange("q (j p u) -> q j p u", j=PACK, u=2)
-            for b in range(2):
-                tp = ps_t.tile([P, 4, P], F32, name="tp", tag="tp")
-                for jj in range(2):
-                    j = 2 * b + jj
-                    for u in range(2):
-                        nc.tensor.transpose(tp[:, 2 * jj + u, :], words[:, 256 * j + u : 256 * (j + 1) : 2], ident[:])
-                nc.scalar.copy(out=grp_w[:, 2 * b : 2 * b + 2, :, :], in_=tp[:].rearrange("q (j u) p -> q j p u", u=2))
-            return grp
-
-        def stage_g(g):
-            dk = keep.tile([P, WIDE], BF16, name="dk%d" % g)
-            nc.vector.tensor_tensor(out=dk[:], in0=go_r[g][:], in1=v_r[g][:], op=MULT)
-            dv = keep.tile([P, WIDE], BF16, name="dv%d" % g)
-            nc.vector.tensor_tensor(out=dv[:], in0=go_r[g][:], in1=k_r[g][:], op=MULT)
-            gk = transposed(dk)
-            gv = transposed(dv)
-            dkt.append(quantize(gk, E5M2, "dkt%d" % g))
-            dvt.append(quantize(gv, E5M2, "dvt%d" % g))
-            gi = interleave("S", dk[:].rearrange("p (j w) -> p j w", j=PACK))
-            dki.append(quantize(gi, E5M2, "dki%d" % g))
-
-        wk_q, wv_q = [], []
-
-        def stage_w(c):
-            eng = "V" if c < 2 else "S"
-            cols = slice(c * N_TILE, (c + 1) * N_TILE)
-            ga = interleave(eng, wk_r[:, :, cols])
-            gb = interleave(eng, wv_r[:, :, cols])
-            wk_q.append(quantize(ga, E4M3, "wk%d" % c))
-            wv_q.append(quantize(gb, E4M3, "wv%d" % c))
-
-        x_q = {}
-
-        def stage_x(g, c):
-            cols = slice(c * N_TILE, (c + 1) * N_TILE)
-            gx = interleave("V", x_r[g][:, :, cols])
-            x_q[(g, c)] = quantize(gx, E4M3, "x%d_%d" % (g, c))
+            tp = ps_x.tile([P, 4, P], F32, name="tp", tag="aux")
+            for jj in range(2):
+                j = 2 * b + jj
+                for u in range(2):
+                    nc.tensor.transpose(tp[:, 2 * jj + u, :], words[:, 256 * j + u : 256 * (j + 1) : 2], ident[:])
+            nc.scalar.copy(out=grp_w[:, 2 * b : 2 * b + 2, :, :], in_=tp[:].rearrange("q (j u) p -> q j p u", u=2))
 
         def mx(acc, a, m, b, start, stop):
             mc = slice(m * P, (m + 1) * P)
@@ -148,33 +136,124 @@ def tile_parallelretention_pa_v_kernel(tc, x, Wk, bk, Wv, bv, K, V, grad_out, ou
                 stop=stop,
             )
 
-        def out0_rows(g, j):
-            st = slabs.tile([P, E], F32, name="st", tag="slab")
-            for c in range(NCH):
-                acc = ps_a.tile([P, N_TILE], F32, name="acc", tag="acc")
-                mx(acc, dkt[g], j, wk_q[c], True, False)
-                mx(acc, dvt[g], j, wv_q[c], False, True)
-                copy_on("S", st[:, c * N_TILE : (c + 1) * N_TILE], acc[:])
-            nc.sync.dma_start(out=o0_v[g, j], in_=st[:])
+        def empty(eng, out, acc):
+            if eng == "V":
+                nc.vector.tensor_copy(out=out, in_=acc[:])
+            else:
+                nc.scalar.copy(out=out, in_=acc[:])
 
-        def out1_rows(m, h):
-            st = slabs.tile([P, E // 2], F32, name="st", tag="slab")
-            for cc in range(2):
-                c = 2 * h + cc
-                acc = ps_a.tile([P, N_TILE], F32, name="acc", tag="acc")
-                mx(acc, dki[0], m, x_q[(0, c)], True, False)
-                mx(acc, dki[1], m, x_q[(1, c)], False, True)
-                copy_on("V" if cc == 1 else "S", st[:, cc * N_TILE : (cc + 1) * N_TILE], acc[:])
-            nc.sync.dma_start(out=o1_v[m][:, h * (E // 2) : (h + 1) * (E // 2)], in_=st[:])
+        dkt, dvt, dki, w_q, x_q = {}, {}, {}, {}, {}
+        rows0, rows1 = {}, {}
 
-        stage_g(0)
-        for c in range(NCH):
-            stage_w(c)
-        stage_g(1)
-        for g in range(G):
-            for j in range(PACK):
-                out0_rows(g, j)
-                stage_x(j % 2, 2 * g + j // 2)
-        for h in range(2):
-            for m in range(NMB):
-                out1_rows(m, h)
+        def out0_tile(g, j, c, eng):
+            if (g, j) not in rows0:
+                rows0[(g, j)] = slabs.tile([P, E], F32, name="st", tag="slab")
+            acc = ps_a.tile([P, N_TILE], F32, name="acc", tag="acc")
+            mx(acc, dkt[g], j, w_q[("k", c)], True, False)
+            mx(acc, dvt[g], j, w_q[("v", c)], False, True)
+            empty(eng, rows0[(g, j)][:, c * N_TILE : (c + 1) * N_TILE], acc)
+
+        def out0_store(g, j):
+            nc.sync.dma_start(out=o0_v[g, j], in_=rows0[(g, j)][:])
+
+        def out1_tile(m, c, eng):
+            if m not in rows1:
+                rows1[m] = slabs.tile([P, E], F32, name="st", tag="slab")
+            acc = ps_a.tile([P, N_TILE], F32, name="acc", tag="acc")
+            mx(acc, dki[0], m, x_q[(0, c)], True, False)
+            mx(acc, dki[1], m, x_q[(1, c)], False, True)
+            empty(eng, rows1[m][:, c * N_TILE : (c + 1) * N_TILE], acc)
+
+        def out1_store(m, h):
+            nc.sync.dma_start(out=o1_v[m][:, h * EH : (h + 1) * EH], in_=rows1[m][:, h * EH : (h + 1) * EH])
+
+        def w_src(w, c):
+            return w_r[(w, c // 2)][:, :, (c % 2) * N_TILE : (c % 2 + 1) * N_TILE]
+
+        def x_src(g, c):
+            return x_r[g][:, :, c * N_TILE : (c + 1) * N_TILE]
+
+        dk0 = keep.tile([P, WIDE], BF16, name="dk0")
+        dv0 = keep.tile([P, WIDE], BF16, name="dv0")
+        gk0 = new_grp()
+        for b in range(2):
+            cols = slice(b * HALF, (b + 1) * HALF)
+            nc.vector.tensor_tensor(out=dk0[:, cols], in0=go_r[(0, b)][:], in1=v_r[(0, b)][:], op=MULT)
+            transpose_half(dk0, gk0, b)
+        gi0 = interleave_pe(dk0[:].rearrange("p (j w) -> p j w", j=PACK))
+        gv0 = new_grp()
+        for b in range(2):
+            cols = slice(b * HALF, (b + 1) * HALF)
+            nc.vector.tensor_tensor(out=dv0[:, cols], in0=go_r[(0, b)][:], in1=k_r[(0, b)][:], op=MULT)
+            transpose_half(dv0, gv0, b)
+        dkt[0] = quantize(gk0, E5M2, "dkt0")
+
+        g_k1 = interleave_pe(w_src("k", 1))
+        g_k0 = interleave_v(w_src("k", 0))
+        dki[0] = quantize(gi0, E5M2, "dki0")
+        dvt[0] = quantize(gv0, E5M2, "dvt0")
+        g_v1 = interleave_pe(w_src("v", 1))
+        g_v0 = interleave_v(w_src("v", 0))
+        w_q[("k", 0)] = quantize(g_k0, E4M3, "wk0")
+        w_q[("k", 1)] = quantize(g_k1, E4M3, "wk1")
+        g_k3 = interleave_pe(w_src("k", 3))
+        g_k2 = interleave_v(w_src("k", 2))
+        w_q[("v", 0)] = quantize(g_v0, E4M3, "wv0")
+        w_q[("v", 1)] = quantize(g_v1, E4M3, "wv1")
+        g_v3 = interleave_pe(w_src("v", 3))
+        for j in range(PACK):
+            for c in (0, 1):
+                out0_tile(0, j, c, "S")
+        g_v2 = interleave_v(w_src("v", 2))
+        w_q[("k", 2)] = quantize(g_k2, E4M3, "wk2")
+        w_q[("k", 3)] = quantize(g_k3, E4M3, "wk3")
+        w_q[("v", 2)] = quantize(g_v2, E4M3, "wv2")
+        w_q[("v", 3)] = quantize(g_v3, E4M3, "wv3")
+
+        dk1 = keep.tile([P, WIDE], BF16, name="dk1")
+        dv1 = keep.tile([P, WIDE], BF16, name="dv1")
+        nc.vector.tensor_tensor(out=dk1[:], in0=go1[:], in1=v1[:], op=MULT)
+        gk1 = new_grp()
+        transpose_half(dk1, gk1, 0)
+        transpose_half(dk1, gk1, 1)
+        for j in (0, 1):
+            for c in (2, 3):
+                out0_tile(0, j, c, "S")
+            out0_store(0, j)
+        nc.vector.tensor_tensor(out=dv1[:], in0=go1[:], in1=k1[:], op=MULT)
+        gv1 = new_grp()
+        transpose_half(dv1, gv1, 0)
+        transpose_half(dv1, gv1, 1)
+        for j in (2, 3):
+            for c in (2, 3):
+                out0_tile(0, j, c, "S")
+            out0_store(0, j)
+
+        order = [(0, 0), (0, 1), (1, 0), (1, 1), (0, 2), (1, 2), (0, 3), (1, 3)]
+        gx = {}
+        gx[order[0]] = interleave_v(x_src(0, 0))
+        dkt[1] = quantize(gk1, E5M2, "dkt1")
+        gx[order[1]] = interleave_v(x_src(0, 1))
+        dvt[1] = quantize(gv1, E5M2, "dvt1")
+        x_q[order[0]] = quantize(gx[order[0]], E4M3, "x0_0")
+        gi1 = interleave_v(dk1[:].rearrange("p (j w) -> p j w", j=PACK))
+        x_q[order[1]] = quantize(gx[order[1]], E4M3, "x0_1")
+        gx[order[2]] = interleave_v(x_src(1, 0))
+        dki[1] = quantize(gi1, E5M2, "dki1")
+        for i in range(3, 8):
+            gx[order[i]] = interleave_v(x_src(order[i][0], order[i][1]))
+            x_q[order[i - 1]] = quantize(gx[order[i - 1]], E4M3, "x%d_%d" % order[i - 1])
+            if i == 4:
+                for j in range(PACK):
+                    for c in range(NCH):
+                        out0_tile(1, j, c, "S")
+                    out0_store(1, j)
+                for m in range(NMB):
+                    for c in (0, 1):
+                        out1_tile(m, c, "S")
+                    out1_store(m, 0)
+        x_q[order[7]] = quantize(gx[order[7]], E4M3, "x%d_%d" % order[7])
+        for m in range(NMB):
+            out1_tile(m, 2, "S")
+            out1_tile(m, 3, "V")
+            out1_store(m, 1)

@@ -35,39 +35,35 @@ def tile_parallelretention_pa_v_kernel(tc, x, Wk, bk, Wv, bv, K, V, grad_out, ou
     k_v = K.flatten_outer_dims().rearrange("(g p j) w -> g p (j w)", g=G, j=PACK)
     v_v = V.flatten_outer_dims().rearrange("(g p j) w -> g p (j w)", g=G, j=PACK)
     w_v = {"k": Wk.rearrange("(p j) e -> p j e", j=PACK), "v": Wv.rearrange("(p j) e -> p j e", j=PACK)}
-    o0_v = out_0.flatten_outer_dims().rearrange("(g p j) e -> g j p e", g=G, j=PACK)
-    o1_v = out_1.rearrange("(m p) e -> m p e", p=P)
+    o0_v = out_0.flatten_outer_dims().rearrange("(g p b i) e -> g b p i e", g=G, b=2, i=2)
+    o1_v = out_1.rearrange("(a i p) e -> a p i e", a=2, i=2)
 
     with ExitStack() as ctx:
         keep = ctx.enter_context(tc.tile_pool(name="keep", bufs=1))
-        slabs = ctx.enter_context(tc.tile_pool(name="slabs", bufs=9))
-        grps = ctx.enter_context(tc.tile_pool(name="grps", bufs=6))
+        bigs = ctx.enter_context(tc.tile_pool(name="bigs", bufs=5))
+        grps = ctx.enter_context(tc.tile_pool(name="grps", bufs=5))
         ps_x = ctx.enter_context(tc.psum_pool(name="ps_x", bufs=3))
         ps_a = ctx.enter_context(tc.psum_pool(name="ps_a", bufs=5))
         ctx.enter_context(tc.manual_schedule())
 
-        go_r, v_r, k_r = {}, {}, {}
+        go0 = keep.tile([P, WIDE], BF16, name="go0")
+        nc.sync.dma_start(out=go0[:], in_=go_v[0])
+        v0 = keep.tile([P, WIDE], F32, name="v0")
         for b in range(2):
-            cols = slice(b * HALF, (b + 1) * HALF)
-            go_r[(0, b)] = keep.tile([P, HALF], BF16, name="go0%d" % b)
-            nc.sync.dma_start(out=go_r[(0, b)][:], in_=go_v[0][:, cols])
-            v_r[(0, b)] = keep.tile([P, HALF], F32, name="v0%d" % b)
-            nc.sync.dma_start(out=v_r[(0, b)][:], in_=v_v[0][:, cols])
-        for b in range(2):
-            cols = slice(b * HALF, (b + 1) * HALF)
-            k_r[(0, b)] = keep.tile([P, HALF], F32, name="k0%d" % b)
-            nc.sync.dma_start(out=k_r[(0, b)][:], in_=k_v[0][:, cols])
+            nc.sync.dma_start(out=v0[:, b * HALF : (b + 1) * HALF], in_=v_v[0][:, b * HALF : (b + 1) * HALF])
+        k0 = keep.tile([P, WIDE], F32, name="k0")
+        nc.sync.dma_start(out=k0[:], in_=k_v[0])
         w_r = {}
+        for w in ("k", "v"):
+            w_r[w] = bigs.tile([P, 2, PACK, EH], BF16, name="w_r", tag="big")
         for h in range(2):
             for w in ("k", "v"):
-                w_r[(w, h)] = slabs.tile([P, PACK, EH], BF16, name="w_r", tag="slab")
-                nc.sync.dma_start(out=w_r[(w, h)][:], in_=w_v[w][:, :, h * EH : (h + 1) * EH])
+                nc.sync.dma_start(out=w_r[w][:, h], in_=w_v[w][:, :, h * EH : (h + 1) * EH])
         go1 = keep.tile([P, WIDE], BF16, name="go1")
         nc.sync.dma_start(out=go1[:], in_=go_v[1])
-        v1 = slabs.tile([P, WIDE], F32, name="v1", tag="slab")
-        nc.sync.dma_start(out=v1[:], in_=v_v[1])
-        k1 = slabs.tile([P, WIDE], F32, name="k1", tag="slab")
-        nc.sync.dma_start(out=k1[:], in_=k_v[1])
+        vk1 = bigs.tile([P, 2, WIDE], F32, name="vk1", tag="big")
+        nc.sync.dma_start(out=vk1[:, 0, :], in_=v_v[1])
+        nc.sync.dma_start(out=vk1[:, 1, :], in_=k_v[1])
         x_r = []
         for g in range(G):
             xr = keep.tile([P, PACK, E], BF16, name="x_r%d" % g)
@@ -146,29 +142,29 @@ def tile_parallelretention_pa_v_kernel(tc, x, Wk, bk, Wv, bv, K, V, grad_out, ou
         rows0, rows1 = {}, {}
 
         def out0_tile(g, j, c, eng):
-            if (g, j) not in rows0:
-                rows0[(g, j)] = slabs.tile([P, E], F32, name="st", tag="slab")
+            if (g, j // 2) not in rows0:
+                rows0[(g, j // 2)] = bigs.tile([P, 2, E], F32, name="st", tag="big")
             acc = ps_a.tile([P, N_TILE], F32, name="acc", tag="acc")
             mx(acc, dkt[g], j, w_q[("k", c)], True, False)
             mx(acc, dvt[g], j, w_q[("v", c)], False, True)
-            empty(eng, rows0[(g, j)][:, c * N_TILE : (c + 1) * N_TILE], acc)
+            empty(eng, rows0[(g, j // 2)][:, j % 2, c * N_TILE : (c + 1) * N_TILE], acc)
 
-        def out0_store(g, j):
-            nc.sync.dma_start(out=o0_v[g, j], in_=rows0[(g, j)][:])
+        def out0_store(g, b):
+            nc.sync.dma_start(out=o0_v[g, b], in_=rows0[(g, b)][:])
 
         def out1_tile(m, c, eng):
-            if m not in rows1:
-                rows1[m] = slabs.tile([P, E], F32, name="st", tag="slab")
+            if m // 2 not in rows1:
+                rows1[m // 2] = bigs.tile([P, 2, 2, EH], F32, name="st", tag="big")
             acc = ps_a.tile([P, N_TILE], F32, name="acc", tag="acc")
             mx(acc, dki[0], m, x_q[(0, c)], True, False)
             mx(acc, dki[1], m, x_q[(1, c)], False, True)
-            empty(eng, rows1[m][:, c * N_TILE : (c + 1) * N_TILE], acc)
+            empty(eng, rows1[m // 2][:, c // 2, m % 2, (c % 2) * N_TILE : (c % 2 + 1) * N_TILE], acc)
 
-        def out1_store(m, h):
-            nc.sync.dma_start(out=o1_v[m][:, h * EH : (h + 1) * EH], in_=rows1[m][:, h * EH : (h + 1) * EH])
+        def out1_store(a, h):
+            nc.sync.dma_start(out=o1_v[a][:, :, h * EH : (h + 1) * EH], in_=rows1[a][:, h])
 
         def w_src(w, c):
-            return w_r[(w, c // 2)][:, :, (c % 2) * N_TILE : (c % 2 + 1) * N_TILE]
+            return w_r[w][:, c // 2, :, (c % 2) * N_TILE : (c % 2 + 1) * N_TILE]
 
         def x_src(g, c):
             return x_r[g][:, :, c * N_TILE : (c + 1) * N_TILE]
@@ -178,61 +174,58 @@ def tile_parallelretention_pa_v_kernel(tc, x, Wk, bk, Wv, bv, K, V, grad_out, ou
         gk0 = new_grp()
         for b in range(2):
             cols = slice(b * HALF, (b + 1) * HALF)
-            nc.vector.tensor_tensor(out=dk0[:, cols], in0=go_r[(0, b)][:], in1=v_r[(0, b)][:], op=MULT)
+            nc.vector.tensor_tensor(out=dk0[:, cols], in0=go0[:, cols], in1=v0[:, cols], op=MULT)
             transpose_half(dk0, gk0, b)
         gi0 = interleave_pe(dk0[:].rearrange("p (j w) -> p j w", j=PACK))
         gv0 = new_grp()
         for b in range(2):
             cols = slice(b * HALF, (b + 1) * HALF)
-            nc.vector.tensor_tensor(out=dv0[:, cols], in0=go_r[(0, b)][:], in1=k_r[(0, b)][:], op=MULT)
+            nc.vector.tensor_tensor(out=dv0[:, cols], in0=go0[:, cols], in1=k0[:, cols], op=MULT)
             transpose_half(dv0, gv0, b)
         dkt[0] = quantize(gk0, E5M2, "dkt0")
 
-        g_k1 = interleave_pe(w_src("k", 1))
-        g_k0 = interleave_v(w_src("k", 0))
+        gw = {}
+        gw[("k", 1)] = interleave_pe(w_src("k", 1))
+        gw[("k", 0)] = interleave_v(w_src("k", 0))
         dki[0] = quantize(gi0, E5M2, "dki0")
         dvt[0] = quantize(gv0, E5M2, "dvt0")
-        g_v1 = interleave_pe(w_src("v", 1))
-        g_v0 = interleave_v(w_src("v", 0))
-        w_q[("k", 0)] = quantize(g_k0, E4M3, "wk0")
-        w_q[("k", 1)] = quantize(g_k1, E4M3, "wk1")
-        g_k3 = interleave_pe(w_src("k", 3))
-        g_k2 = interleave_v(w_src("k", 2))
-        w_q[("v", 0)] = quantize(g_v0, E4M3, "wv0")
-        w_q[("v", 1)] = quantize(g_v1, E4M3, "wv1")
-        g_v3 = interleave_pe(w_src("v", 3))
+        for h in range(2):
+            gw[("v", 2 * h + 1)] = interleave_pe(w_src("v", 2 * h + 1))
+            gw[("v", 2 * h)] = interleave_v(w_src("v", 2 * h))
+            for c in (2 * h, 2 * h + 1):
+                w_q[("k", c)] = quantize(gw[("k", c)], E4M3, "wk%d" % c)
+            if h == 0:
+                gw[("k", 3)] = interleave_pe(w_src("k", 3))
+                gw[("k", 2)] = interleave_v(w_src("k", 2))
+            for c in (2 * h, 2 * h + 1):
+                w_q[("v", c)] = quantize(gw[("v", c)], E4M3, "wv%d" % c)
         for j in range(PACK):
             for c in (0, 1):
                 out0_tile(0, j, c, "S")
-        g_v2 = interleave_v(w_src("v", 2))
-        w_q[("k", 2)] = quantize(g_k2, E4M3, "wk2")
-        w_q[("k", 3)] = quantize(g_k3, E4M3, "wk3")
-        w_q[("v", 2)] = quantize(g_v2, E4M3, "wv2")
-        w_q[("v", 3)] = quantize(g_v3, E4M3, "wv3")
 
         dk1 = keep.tile([P, WIDE], BF16, name="dk1")
         dv1 = keep.tile([P, WIDE], BF16, name="dv1")
-        nc.vector.tensor_tensor(out=dk1[:], in0=go1[:], in1=v1[:], op=MULT)
+        nc.vector.tensor_tensor(out=dk1[:], in0=go1[:], in1=vk1[:, 0, :], op=MULT)
         gk1 = new_grp()
         transpose_half(dk1, gk1, 0)
         transpose_half(dk1, gk1, 1)
         for j in (0, 1):
             for c in (2, 3):
                 out0_tile(0, j, c, "S")
-            out0_store(0, j)
-        nc.vector.tensor_tensor(out=dv1[:], in0=go1[:], in1=k1[:], op=MULT)
+        out0_store(0, 0)
+        nc.vector.tensor_tensor(out=dv1[:], in0=go1[:], in1=vk1[:, 1, :], op=MULT)
         gv1 = new_grp()
         transpose_half(dv1, gv1, 0)
         transpose_half(dv1, gv1, 1)
         for j in (2, 3):
             for c in (2, 3):
                 out0_tile(0, j, c, "S")
-            out0_store(0, j)
+        out0_store(0, 1)
 
         order = [(0, 0), (0, 1), (1, 0), (1, 1), (0, 2), (1, 2), (0, 3), (1, 3)]
         gx = {}
-        gx[order[0]] = interleave_v(x_src(0, 0))
         dkt[1] = quantize(gk1, E5M2, "dkt1")
+        gx[order[0]] = interleave_v(x_src(0, 0))
         gx[order[1]] = interleave_v(x_src(0, 1))
         dvt[1] = quantize(gv1, E5M2, "dvt1")
         x_q[order[0]] = quantize(gx[order[0]], E4M3, "x0_0")
@@ -247,13 +240,18 @@ def tile_parallelretention_pa_v_kernel(tc, x, Wk, bk, Wv, bv, K, V, grad_out, ou
                 for j in range(PACK):
                     for c in range(NCH):
                         out0_tile(1, j, c, "S")
-                    out0_store(1, j)
+                    if j % 2 == 1:
+                        out0_store(1, j // 2)
                 for m in range(NMB):
                     for c in (0, 1):
                         out1_tile(m, c, "S")
-                    out1_store(m, 0)
+                    if m % 2 == 1:
+                        out1_store(m // 2, 0)
+            if i == 6:
+                for m in range(NMB):
+                    out1_tile(m, 2, "S")
         x_q[order[7]] = quantize(gx[order[7]], E4M3, "x%d_%d" % order[7])
         for m in range(NMB):
-            out1_tile(m, 2, "S")
-            out1_tile(m, 3, "V")
-            out1_store(m, 1)
+            out1_tile(m, 3, "V" if m % 2 == 0 else "S")
+            if m % 2 == 1:
+                out1_store(m // 2, 1)

@@ -11,17 +11,18 @@ E4M3 = mybir.dt.float8_e4m3fn_x4
 E5M2 = mybir.dt.float8_e5m2_x4
 MULT = mybir.AluOpType.mult
 
+T, QD, E = 1024, 512, 2048
+
 P = 128
 PACK = 4
-T, QD, E = 1024, 512, 2048
 K_PASS = P * PACK
-G = T // K_PASS
+PASSES = T // K_PASS
 N_TILE = 512
-NCH = E // N_TILE
-NMB = QD // P
-WIDE = PACK * N_TILE
-HALF = WIDE // 2
-EH = E // 2
+CHUNKS = E // N_TILE
+FEATURE_TILES = QD // P
+GROUPED = PACK * N_TILE
+HALF = GROUPED // 2
+E_HALF = E // 2
 
 FLOPS = 2 * T * QD * E * 3
 BYTES = 2 * (T * E + 2 * QD * E + T * QD) + 4 * (2 * T * QD) + 4 * (T * E + QD * E)
@@ -30,13 +31,13 @@ BYTES = 2 * (T * E + 2 * QD * E + T * QD) + 4 * (2 * T * QD) + 4 * (T * E + QD *
 def tile_parallelretention_pa_v_kernel(tc, x, Wk, bk, Wv, bv, K, V, grad_out, out_0, out_1):
     nc = tc.nc
 
-    x_v = x.flatten_outer_dims().rearrange("(g p j) e -> g p j e", g=G, j=PACK)
-    go_v = grad_out.flatten_outer_dims().rearrange("(g p j) w -> g p (j w)", g=G, j=PACK)
-    k_v = K.flatten_outer_dims().rearrange("(g p j) w -> g p (j w)", g=G, j=PACK)
-    v_v = V.flatten_outer_dims().rearrange("(g p j) w -> g p (j w)", g=G, j=PACK)
-    w_v = {"k": Wk.rearrange("(p j) e -> p j e", j=PACK), "v": Wv.rearrange("(p j) e -> p j e", j=PACK)}
-    o0_v = out_0.flatten_outer_dims().rearrange("(g p b i) e -> g b p i e", g=G, b=2, i=2)
-    o1_v = out_1.rearrange("(a i p) e -> a p i e", a=2, i=2)
+    x_hbm = x.flatten_outer_dims().rearrange("(g p j) e -> g p j e", g=PASSES, j=PACK)
+    grad_hbm = grad_out.flatten_outer_dims().rearrange("(g p j) w -> g p (j w)", g=PASSES, j=PACK)
+    k_hbm = K.flatten_outer_dims().rearrange("(g p j) w -> g p (j w)", g=PASSES, j=PACK)
+    v_hbm = V.flatten_outer_dims().rearrange("(g p j) w -> g p (j w)", g=PASSES, j=PACK)
+    w_hbm = {"k": Wk.rearrange("(p j) e -> p j e", j=PACK), "v": Wv.rearrange("(p j) e -> p j e", j=PACK)}
+    out0_hbm = out_0.flatten_outer_dims().rearrange("(g p b i) e -> g b p i e", g=PASSES, b=2, i=2)
+    out1_hbm = out_1.rearrange("(a i p) e -> a p i e", a=2, i=2)
 
     with ExitStack() as ctx:
         keep = ctx.enter_context(tc.tile_pool(name="keep", bufs=1))
@@ -46,212 +47,228 @@ def tile_parallelretention_pa_v_kernel(tc, x, Wk, bk, Wv, bv, K, V, grad_out, ou
         ps_a = ctx.enter_context(tc.psum_pool(name="ps_a", bufs=5))
         ctx.enter_context(tc.manual_schedule())
 
-        go0 = keep.tile([P, WIDE], BF16, name="go0")
-        nc.sync.dma_start(out=go0[:], in_=go_v[0])
-        v0 = keep.tile([P, WIDE], F32, name="v0")
+        grad0 = keep.tile([P, GROUPED], BF16, name="go0")
+        nc.sync.dma_start(out=grad0[:], in_=grad_hbm[0])
+        v0 = keep.tile([P, GROUPED], F32, name="v0")
         for b in range(2):
-            nc.sync.dma_start(out=v0[:, b * HALF : (b + 1) * HALF], in_=v_v[0][:, b * HALF : (b + 1) * HALF])
-        k0 = keep.tile([P, WIDE], F32, name="k0")
-        nc.sync.dma_start(out=k0[:], in_=k_v[0])
-        w_r = {}
+            nc.sync.dma_start(out=v0[:, b * HALF : (b + 1) * HALF], in_=v_hbm[0][:, b * HALF : (b + 1) * HALF])
+        k0 = keep.tile([P, GROUPED], F32, name="k0")
+        nc.sync.dma_start(out=k0[:], in_=k_hbm[0])
+        w_raw = {}
         for w in ("k", "v"):
-            w_r[w] = bigs.tile([P, 2, PACK, EH], BF16, name="w_r", tag="big")
+            w_raw[w] = bigs.tile([P, 2, PACK, E_HALF], BF16, name="w_r", tag="big")
         for h in range(2):
             for w in ("k", "v"):
-                nc.sync.dma_start(out=w_r[w][:, h], in_=w_v[w][:, :, h * EH : (h + 1) * EH])
-        go1 = keep.tile([P, WIDE], BF16, name="go1")
-        nc.sync.dma_start(out=go1[:], in_=go_v[1])
-        vk1 = bigs.tile([P, 2, WIDE], F32, name="vk1", tag="big")
-        nc.sync.dma_start(out=vk1[:, 0, :], in_=v_v[1])
-        nc.sync.dma_start(out=vk1[:, 1, :], in_=k_v[1])
-        x_r = []
-        for g in range(G):
-            xr = keep.tile([P, PACK, E], BF16, name="x_r%d" % g)
-            nc.sync.dma_start(out=xr[:], in_=x_v[g])
-            x_r.append(xr)
+                nc.sync.dma_start(out=w_raw[w][:, h], in_=w_hbm[w][:, :, h * E_HALF : (h + 1) * E_HALF])
+        grad1 = keep.tile([P, GROUPED], BF16, name="go1")
+        nc.sync.dma_start(out=grad1[:], in_=grad_hbm[1])
+        vk1 = bigs.tile([P, 2, GROUPED], F32, name="vk1", tag="big")
+        nc.sync.dma_start(out=vk1[:, 0, :], in_=v_hbm[1])
+        nc.sync.dma_start(out=vk1[:, 1, :], in_=k_hbm[1])
+        x_raw = []
+        for g in range(PASSES):
+            x_pass = keep.tile([P, PACK, E], BF16, name="x_r%d" % g)
+            nc.sync.dma_start(out=x_pass[:], in_=x_hbm[g])
+            x_raw.append(x_pass)
 
-        ident = keep.tile([P, P], F32, name="ident")
-        make_identity(nc, ident[:])
-        ident_b = keep.tile([P, P], BF16, name="ident_b")
-        make_identity(nc, ident_b[:])
-        warm = keep.tile([P, 8], F32, name="warm")
-        nc.vector.memset(warm[:], 0.0)
-        warm2 = keep.tile([P, 8], F32, name="warm2")
-        nc.scalar.copy(out=warm2[:], in_=warm[:])
+        ident_f32 = keep.tile([P, P], F32, name="ident")
+        make_identity(nc, ident_f32[:])
+        ident_bf16 = keep.tile([P, P], BF16, name="ident_b")
+        make_identity(nc, ident_bf16[:])
+        warm_in = keep.tile([P, 8], F32, name="warm")
+        nc.vector.memset(warm_in[:], 0.0)
+        warm_out = keep.tile([P, 8], F32, name="warm2")
+        nc.scalar.copy(out=warm_out[:], in_=warm_in[:])
 
-        def new_grp():
-            grp = grps.tile([P, WIDE], BF16, name="grp", tag="grp", align_bytes=64)
-            return grp
+        def new_grouped():
+            grouped = grps.tile([P, GROUPED], BF16, name="grp", tag="grp", align_bytes=64)
+            return grouped
 
-        def quantize(grp, fmt, name):
+        def quantize(grouped, fmt, name):
             codes = keep.tile([P, N_TILE], U32, name=name + "_c", align_bytes=64)
             scales = keep.tile([P, N_TILE], U8, name=name + "_s", align_bytes=64)
-            nc.vector.quantize_mx(out=codes[:].bitcast(fmt), scales=scales[:], in_=grp[:])
+            nc.vector.quantize_mx(out=codes[:].bitcast(fmt), scales=scales[:], in_=grouped[:])
             return codes, scales
 
-        def interleave_v(src_pjw):
-            grp = new_grp()
-            nc.vector.tensor_copy(out=grp[:].rearrange("p (w j) -> p w j", j=PACK), in_=src_pjw.rearrange("p j w -> p w j"))
-            return grp
+        def interleave_on_vector(rows):
+            grouped = new_grouped()
+            nc.vector.tensor_copy(
+                out=grouped[:].rearrange("p (c i j) -> p c j i", i=4, j=PACK), in_=rows.rearrange("p j (c i) -> p c j i", i=4)
+            )
+            return grouped
 
-        def interleave_pe(src_pjw):
-            grp = new_grp()
-            for hb in range(2):
-                mv = ps_x.tile([P, 2 * N_TILE], BF16, name="mv", tag="aux")
-                for q in range(2):
-                    c0 = hb * 256 + q * P
+        def interleave_on_tensor(rows):
+            grouped = new_grouped()
+            for bank in range(2):
+                moved = ps_x.tile([P, 2 * N_TILE], BF16, name="mv", tag="aux")
+                for part in range(2):
+                    first = bank * 2 * P + part * P
                     nc.tensor.matmul(
-                        out=mv[:, q * N_TILE : (q + 1) * N_TILE],
-                        lhsT=ident_b[:],
-                        rhs=src_pjw[:, :, c0 : c0 + P].rearrange("p j w -> p w j"),
+                        out=moved[:, part * N_TILE : (part + 1) * N_TILE],
+                        lhsT=ident_bf16[:],
+                        rhs=rows[:, :, first : first + P].rearrange("p j w -> p w j"),
                         start=True,
                         stop=True,
                     )
-                nc.scalar.copy(out=grp[:, hb * HALF : (hb + 1) * HALF], in_=mv[:])
-            return grp
+                nc.scalar.copy(out=grouped[:, bank * HALF : (bank + 1) * HALF], in_=moved[:])
+            return grouped
 
-        def transpose_half(dz, grp, b):
+        def transpose_row_pair(dz, grouped, b):
             words = dz[:].bitcast(F32)
-            grp_w = grp[:].bitcast(F32).rearrange("q (j p u) -> q j p u", j=PACK, u=2)
-            tp = ps_x.tile([P, 4, P], F32, name="tp", tag="aux")
-            for jj in range(2):
-                j = 2 * b + jj
+            grouped_words = grouped[:].bitcast(F32).rearrange("q (j p u) -> q j p u", j=PACK, u=2)
+            turned = ps_x.tile([P, 4, P], F32, name="tp", tag="aux")
+            for i in range(2):
+                j = 2 * b + i
                 for u in range(2):
-                    nc.tensor.transpose(tp[:, 2 * jj + u, :], words[:, 256 * j + u : 256 * (j + 1) : 2], ident[:])
-            nc.scalar.copy(out=grp_w[:, 2 * b : 2 * b + 2, :, :], in_=tp[:].rearrange("q (j u) p -> q j p u", u=2))
+                    nc.tensor.transpose(turned[:, 2 * i + u, :], words[:, 256 * j + u : 256 * (j + 1) : 2], ident_f32[:])
+            nc.scalar.copy(
+                out=grouped_words[:, 2 * b : 2 * b + 2, :, :], in_=turned[:].rearrange("q (j u) p -> q j p u", u=2)
+            )
 
-        def mx(acc, a, m, b, start, stop):
-            mc = slice(m * P, (m + 1) * P)
+        def matmul_mx(acc, stationary, tile_index, moving, start, stop):
+            cols = slice(tile_index * P, (tile_index + 1) * P)
             nc.tensor.matmul_mx(
                 out=acc[:],
-                lhsT=a[0][:, mc].bitcast(E5M2),
-                lhsT_scale=a[1][:, mc],
-                rhs=b[0][:].bitcast(E4M3),
-                rhs_scale=b[1][:],
+                lhsT=stationary[0][:, cols].bitcast(E5M2),
+                lhsT_scale=stationary[1][:, cols],
+                rhs=moving[0][:].bitcast(E4M3),
+                rhs_scale=moving[1][:],
                 start=start,
                 stop=stop,
             )
 
-        def empty(eng, out, acc):
-            if eng == "V":
+        def empty_bank(engine, out, acc):
+            if engine == "vector":
                 nc.vector.tensor_copy(out=out, in_=acc[:])
             else:
                 nc.scalar.copy(out=out, in_=acc[:])
 
-        dkt, dvt, dki, w_q, x_q = {}, {}, {}, {}, {}
-        rows0, rows1 = {}, {}
+        dk_by_feature, dv_by_feature, dk_by_token = {}, {}, {}
+        w_quant, x_quant = {}, {}
+        out0_rows, out1_rows = {}, {}
 
-        def out0_tile(g, j, c, eng):
-            if (g, j // 2) not in rows0:
-                rows0[(g, j // 2)] = bigs.tile([P, 2, E], F32, name="st", tag="big")
+        def out0_tile(g, j, c):
+            if (g, j // 2) not in out0_rows:
+                out0_rows[(g, j // 2)] = bigs.tile([P, 2, E], F32, name="st", tag="big")
             acc = ps_a.tile([P, N_TILE], F32, name="acc", tag="acc")
-            mx(acc, dkt[g], j, w_q[("k", c)], True, False)
-            mx(acc, dvt[g], j, w_q[("v", c)], False, True)
-            empty(eng, rows0[(g, j // 2)][:, j % 2, c * N_TILE : (c + 1) * N_TILE], acc)
+            matmul_mx(acc, dk_by_feature[g], j, w_quant[("k", c)], True, False)
+            matmul_mx(acc, dv_by_feature[g], j, w_quant[("v", c)], False, True)
+            empty_bank("scalar", out0_rows[(g, j // 2)][:, j % 2, c * N_TILE : (c + 1) * N_TILE], acc)
 
         def out0_store(g, b):
-            nc.sync.dma_start(out=o0_v[g, b], in_=rows0[(g, b)][:])
+            nc.sync.dma_start(out=out0_hbm[g, b], in_=out0_rows[(g, b)][:])
 
-        def out1_tile(m, c, eng):
-            if m // 2 not in rows1:
-                rows1[m // 2] = bigs.tile([P, 2, 2, EH], F32, name="st", tag="big")
+        def out1_tile(m, c, engine):
+            if m // 2 not in out1_rows:
+                out1_rows[m // 2] = bigs.tile([P, 2, 2, E_HALF], F32, name="st", tag="big")
             acc = ps_a.tile([P, N_TILE], F32, name="acc", tag="acc")
-            mx(acc, dki[0], m, x_q[(0, c)], True, False)
-            mx(acc, dki[1], m, x_q[(1, c)], False, True)
-            empty(eng, rows1[m // 2][:, c // 2, m % 2, (c % 2) * N_TILE : (c % 2 + 1) * N_TILE], acc)
+            matmul_mx(acc, dk_by_token[0], m, x_quant[(0, c)], True, False)
+            matmul_mx(acc, dk_by_token[1], m, x_quant[(1, c)], False, True)
+            empty_bank(engine, out1_rows[m // 2][:, c // 2, m % 2, (c % 2) * N_TILE : (c % 2 + 1) * N_TILE], acc)
 
         def out1_store(a, h):
-            nc.sync.dma_start(out=o1_v[a][:, :, h * EH : (h + 1) * EH], in_=rows1[a][:, h])
+            nc.sync.dma_start(out=out1_hbm[a][:, :, h * E_HALF : (h + 1) * E_HALF], in_=out1_rows[a][:, h])
 
-        def w_src(w, c):
-            return w_r[w][:, c // 2, :, (c % 2) * N_TILE : (c % 2 + 1) * N_TILE]
+        def w_rows(w, c):
+            return w_raw[w][:, c // 2, :, (c % 2) * N_TILE : (c % 2 + 1) * N_TILE]
 
-        def x_src(g, c):
-            return x_r[g][:, :, c * N_TILE : (c + 1) * N_TILE]
+        def x_rows(g, c):
+            return x_raw[g][:, :, c * N_TILE : (c + 1) * N_TILE]
 
-        dk0 = keep.tile([P, WIDE], BF16, name="dk0")
-        dv0 = keep.tile([P, WIDE], BF16, name="dv0")
-        gk0 = new_grp()
+        def dz_rows(dz):
+            return dz[:].rearrange("p (j w) -> p j w", j=PACK)
+
+        dk0 = keep.tile([P, GROUPED], BF16, name="dk0")
+        dv0 = keep.tile([P, GROUPED], BF16, name="dv0")
+        dk0_turned = new_grouped()
         for b in range(2):
             cols = slice(b * HALF, (b + 1) * HALF)
-            nc.vector.tensor_tensor(out=dk0[:, cols], in0=go0[:, cols], in1=v0[:, cols], op=MULT)
-            transpose_half(dk0, gk0, b)
-        gi0 = interleave_pe(dk0[:].rearrange("p (j w) -> p j w", j=PACK))
-        gv0 = new_grp()
+            nc.vector.tensor_tensor(out=dk0[:, cols], in0=grad0[:, cols], in1=v0[:, cols], op=MULT)
+            transpose_row_pair(dk0, dk0_turned, b)
+        dk0_grouped = interleave_on_tensor(dz_rows(dk0))
+        dv0_turned = new_grouped()
         for b in range(2):
             cols = slice(b * HALF, (b + 1) * HALF)
-            nc.vector.tensor_tensor(out=dv0[:, cols], in0=go0[:, cols], in1=k0[:, cols], op=MULT)
-            transpose_half(dv0, gv0, b)
-        dkt[0] = quantize(gk0, E5M2, "dkt0")
+            nc.vector.tensor_tensor(out=dv0[:, cols], in0=grad0[:, cols], in1=k0[:, cols], op=MULT)
+            transpose_row_pair(dv0, dv0_turned, b)
+        dk_by_feature[0] = quantize(dk0_turned, E5M2, "dkt0")
 
-        gw = {}
-        gw[("k", 1)] = interleave_pe(w_src("k", 1))
-        gw[("k", 0)] = interleave_v(w_src("k", 0))
-        dki[0] = quantize(gi0, E5M2, "dki0")
-        dvt[0] = quantize(gv0, E5M2, "dvt0")
+        w_grouped = {}
+        w_grouped[("k", 1)] = interleave_on_tensor(w_rows("k", 1))
+        w_grouped[("k", 0)] = interleave_on_vector(w_rows("k", 0))
+        dk_by_token[0] = quantize(dk0_grouped, E5M2, "dki0")
+        dv_by_feature[0] = quantize(dv0_turned, E5M2, "dvt0")
         for h in range(2):
-            gw[("v", 2 * h + 1)] = interleave_pe(w_src("v", 2 * h + 1))
-            gw[("v", 2 * h)] = interleave_v(w_src("v", 2 * h))
+            w_grouped[("v", 2 * h + 1)] = interleave_on_tensor(w_rows("v", 2 * h + 1))
+            w_grouped[("v", 2 * h)] = interleave_on_vector(w_rows("v", 2 * h))
             for c in (2 * h, 2 * h + 1):
-                w_q[("k", c)] = quantize(gw[("k", c)], E4M3, "wk%d" % c)
+                w_quant[("k", c)] = quantize(w_grouped[("k", c)], E4M3, "wk%d" % c)
             if h == 0:
-                gw[("k", 3)] = interleave_pe(w_src("k", 3))
-                gw[("k", 2)] = interleave_v(w_src("k", 2))
+                w_grouped[("k", 3)] = interleave_on_tensor(w_rows("k", 3))
+                w_grouped[("k", 2)] = interleave_on_vector(w_rows("k", 2))
             for c in (2 * h, 2 * h + 1):
-                w_q[("v", c)] = quantize(gw[("v", c)], E4M3, "wv%d" % c)
+                w_quant[("v", c)] = quantize(w_grouped[("v", c)], E4M3, "wv%d" % c)
+
         for j in range(PACK):
             for c in (0, 1):
-                out0_tile(0, j, c, "S")
+                out0_tile(0, j, c)
 
-        dk1 = keep.tile([P, WIDE], BF16, name="dk1")
-        dv1 = keep.tile([P, WIDE], BF16, name="dv1")
-        nc.vector.tensor_tensor(out=dk1[:], in0=go1[:], in1=vk1[:, 0, :], op=MULT)
-        gk1 = new_grp()
-        transpose_half(dk1, gk1, 0)
-        transpose_half(dk1, gk1, 1)
+        dk1 = keep.tile([P, GROUPED], BF16, name="dk1")
+        dv1 = keep.tile([P, GROUPED], BF16, name="dv1")
+        nc.vector.tensor_tensor(out=dk1[:], in0=grad1[:], in1=vk1[:, 0, :], op=MULT)
+        dk1_turned = new_grouped()
+        transpose_row_pair(dk1, dk1_turned, 0)
+        transpose_row_pair(dk1, dk1_turned, 1)
         for j in (0, 1):
             for c in (2, 3):
-                out0_tile(0, j, c, "S")
+                out0_tile(0, j, c)
         out0_store(0, 0)
-        nc.vector.tensor_tensor(out=dv1[:], in0=go1[:], in1=vk1[:, 1, :], op=MULT)
-        gv1 = new_grp()
-        transpose_half(dv1, gv1, 0)
-        transpose_half(dv1, gv1, 1)
+        nc.vector.tensor_tensor(out=dv1[:], in0=grad1[:], in1=vk1[:, 1, :], op=MULT)
+        dv1_turned = new_grouped()
+        transpose_row_pair(dv1, dv1_turned, 0)
+        transpose_row_pair(dv1, dv1_turned, 1)
         for j in (2, 3):
             for c in (2, 3):
-                out0_tile(0, j, c, "S")
+                out0_tile(0, j, c)
         out0_store(0, 1)
 
-        order = [(0, 0), (0, 1), (1, 0), (1, 1), (0, 2), (1, 2), (0, 3), (1, 3)]
-        gx = {}
-        dkt[1] = quantize(gk1, E5M2, "dkt1")
-        gx[order[0]] = interleave_v(x_src(0, 0))
-        gx[order[1]] = interleave_v(x_src(0, 1))
-        dvt[1] = quantize(gv1, E5M2, "dvt1")
-        x_q[order[0]] = quantize(gx[order[0]], E4M3, "x0_0")
-        gi1 = interleave_v(dk1[:].rearrange("p (j w) -> p j w", j=PACK))
-        x_q[order[1]] = quantize(gx[order[1]], E4M3, "x0_1")
-        gx[order[2]] = interleave_v(x_src(1, 0))
-        dki[1] = quantize(gi1, E5M2, "dki1")
-        for i in range(3, 8):
-            gx[order[i]] = interleave_v(x_src(order[i][0], order[i][1]))
-            x_q[order[i - 1]] = quantize(gx[order[i - 1]], E4M3, "x%d_%d" % order[i - 1])
-            if i == 4:
-                for j in range(PACK):
-                    for c in range(NCH):
-                        out0_tile(1, j, c, "S")
-                    if j % 2 == 1:
-                        out0_store(1, j // 2)
-                for m in range(NMB):
-                    for c in (0, 1):
-                        out1_tile(m, c, "S")
-                    if m % 2 == 1:
-                        out1_store(m // 2, 0)
-            if i == 6:
-                for m in range(NMB):
-                    out1_tile(m, 2, "S")
-        x_q[order[7]] = quantize(gx[order[7]], E4M3, "x%d_%d" % order[7])
-        for m in range(NMB):
-            out1_tile(m, 3, "V" if m % 2 == 0 else "S")
+        def out0_pass1_then_out1_chunks_0_1():
+            for j in range(PACK):
+                for c in range(CHUNKS):
+                    out0_tile(1, j, c)
+                if j % 2 == 1:
+                    out0_store(1, j // 2)
+            for m in range(FEATURE_TILES):
+                for c in (0, 1):
+                    out1_tile(m, c, "scalar")
+                if m % 2 == 1:
+                    out1_store(m // 2, 0)
+
+        def out1_chunk_2():
+            for m in range(FEATURE_TILES):
+                out1_tile(m, 2, "scalar")
+
+        dk_by_feature[1] = quantize(dk1_turned, E5M2, "dkt1")
+        jobs = [(0, 0), (0, 1), "dk1", (1, 0), (1, 1), (0, 2), (1, 2), (0, 3), (1, 3)]
+        grouped_of = {}
+        for n in range(len(jobs) + 1):
+            if n < len(jobs):
+                job = jobs[n]
+                grouped_of[job] = interleave_on_vector(dz_rows(dk1) if job == "dk1" else x_rows(job[0], job[1]))
+            if n == 1:
+                dv_by_feature[1] = quantize(dv1_turned, E5M2, "dvt1")
+            if n >= 1:
+                job = jobs[n - 1]
+                if job == "dk1":
+                    dk_by_token[1] = quantize(grouped_of[job], E5M2, "dki1")
+                else:
+                    x_quant[job] = quantize(grouped_of[job], E4M3, "x%d_%d" % job)
+                if job == (1, 1):
+                    out0_pass1_then_out1_chunks_0_1()
+                if job == (1, 2):
+                    out1_chunk_2()
+
+        for m in range(FEATURE_TILES):
+            out1_tile(m, 3, "vector" if m % 2 == 0 else "scalar")
             if m % 2 == 1:
                 out1_store(m // 2, 1)

from contextlib import ExitStack

import concourse.mybir as mybir
from concourse.masks import make_identity

F32 = mybir.dt.float32
BF16 = mybir.dt.bfloat16
U32 = mybir.dt.uint32
U8 = mybir.dt.uint8
E4M3 = mybir.dt.float8_e4m3fn_x4
E5M2 = mybir.dt.float8_e5m2_x4
MULT = mybir.AluOpType.mult

T, QD, E = 1024, 512, 2048

P = 128
PACK = 4
K_PASS = P * PACK
PASSES = T // K_PASS
N_TILE = 512
CHUNKS = E // N_TILE
FEATURE_TILES = QD // P
GROUPED = PACK * N_TILE
HALF = GROUPED // 2
E_HALF = E // 2

FLOPS = 2 * T * QD * E * 3
BYTES = 2 * (T * E + 2 * QD * E + T * QD) + 4 * (2 * T * QD) + 4 * (T * E + QD * E)


def tile_parallelretention_pa_v_kernel(tc, x, Wk, bk, Wv, bv, K, V, grad_out, out_0, out_1):
    nc = tc.nc

    x_hbm = x.flatten_outer_dims().rearrange("(g p j) e -> g p j e", g=PASSES, j=PACK)
    grad_hbm = grad_out.flatten_outer_dims().rearrange("(g p j) w -> g p (j w)", g=PASSES, j=PACK)
    k_hbm = K.flatten_outer_dims().rearrange("(g p j) w -> g p (j w)", g=PASSES, j=PACK)
    v_hbm = V.flatten_outer_dims().rearrange("(g p j) w -> g p (j w)", g=PASSES, j=PACK)
    w_hbm = {"k": Wk.rearrange("(p j) e -> p j e", j=PACK), "v": Wv.rearrange("(p j) e -> p j e", j=PACK)}
    out0_hbm = out_0.flatten_outer_dims().rearrange("(g p b i) e -> g b p i e", g=PASSES, b=2, i=2)
    out1_hbm = out_1.rearrange("(a i p) e -> a p i e", a=2, i=2)

    with ExitStack() as ctx:
        keep = ctx.enter_context(tc.tile_pool(name="keep", bufs=1))
        bigs = ctx.enter_context(tc.tile_pool(name="bigs", bufs=5))
        grps = ctx.enter_context(tc.tile_pool(name="grps", bufs=5))
        ps_x = ctx.enter_context(tc.psum_pool(name="ps_x", bufs=3))
        ps_a = ctx.enter_context(tc.psum_pool(name="ps_a", bufs=5))
        ctx.enter_context(tc.manual_schedule())

        grad0 = keep.tile([P, GROUPED], BF16, name="go0")
        nc.sync.dma_start(out=grad0[:], in_=grad_hbm[0])
        v0 = keep.tile([P, GROUPED], F32, name="v0")
        for b in range(2):
            nc.sync.dma_start(out=v0[:, b * HALF : (b + 1) * HALF], in_=v_hbm[0][:, b * HALF : (b + 1) * HALF])
        k0 = keep.tile([P, GROUPED], F32, name="k0")
        nc.sync.dma_start(out=k0[:], in_=k_hbm[0])
        w_raw = {}
        for w in ("k", "v"):
            w_raw[w] = bigs.tile([P, 2, PACK, E_HALF], BF16, name="w_r", tag="big")
        for h in range(2):
            for w in ("k", "v"):
                nc.sync.dma_start(out=w_raw[w][:, h], in_=w_hbm[w][:, :, h * E_HALF : (h + 1) * E_HALF])
        grad1 = keep.tile([P, GROUPED], BF16, name="go1")
        nc.sync.dma_start(out=grad1[:], in_=grad_hbm[1])
        vk1 = bigs.tile([P, 2, GROUPED], F32, name="vk1", tag="big")
        nc.sync.dma_start(out=vk1[:, 0, :], in_=v_hbm[1])
        nc.sync.dma_start(out=vk1[:, 1, :], in_=k_hbm[1])
        x_raw = []
        for g in range(PASSES):
            x_pass = keep.tile([P, PACK, E], BF16, name="x_r%d" % g)
            nc.sync.dma_start(out=x_pass[:], in_=x_hbm[g])
            x_raw.append(x_pass)

        ident_f32 = keep.tile([P, P], F32, name="ident")
        make_identity(nc, ident_f32[:])
        ident_bf16 = keep.tile([P, P], BF16, name="ident_b")
        make_identity(nc, ident_bf16[:])
        warm_in = keep.tile([P, 8], F32, name="warm")
        nc.vector.memset(warm_in[:], 0.0)
        warm_out = keep.tile([P, 8], F32, name="warm2")
        nc.scalar.copy(out=warm_out[:], in_=warm_in[:])

        def new_grouped():
            grouped = grps.tile([P, GROUPED], BF16, name="grp", tag="grp", align_bytes=64)
            return grouped

        def quantize(grouped, fmt, name):
            codes = keep.tile([P, N_TILE], U32, name=name + "_c", align_bytes=64)
            scales = keep.tile([P, N_TILE], U8, name=name + "_s", align_bytes=64)
            nc.vector.quantize_mx(out=codes[:].bitcast(fmt), scales=scales[:], in_=grouped[:])
            return codes, scales

        def interleave_on_vector(rows):
            grouped = new_grouped()
            nc.vector.tensor_copy(
                out=grouped[:].rearrange("p (c i j) -> p c j i", i=4, j=PACK), in_=rows.rearrange("p j (c i) -> p c j i", i=4)
            )
            return grouped

        def interleave_on_tensor(rows):
            grouped = new_grouped()
            for bank in range(2):
                moved = ps_x.tile([P, 2 * N_TILE], BF16, name="mv", tag="aux")
                for part in range(2):
                    first = bank * 2 * P + part * P
                    nc.tensor.matmul(
                        out=moved[:, part * N_TILE : (part + 1) * N_TILE],
                        lhsT=ident_bf16[:],
                        rhs=rows[:, :, first : first + P].rearrange("p j w -> p w j"),
                        start=True,
                        stop=True,
                    )
                nc.scalar.copy(out=grouped[:, bank * HALF : (bank + 1) * HALF], in_=moved[:])
            return grouped

        def transpose_row_pair(dz, grouped, b):
            words = dz[:].bitcast(F32)
            grouped_words = grouped[:].bitcast(F32).rearrange("q (j p u) -> q j p u", j=PACK, u=2)
            turned = ps_x.tile([P, 4, P], F32, name="tp", tag="aux")
            for i in range(2):
                j = 2 * b + i
                for u in range(2):
                    nc.tensor.transpose(turned[:, 2 * i + u, :], words[:, 256 * j + u : 256 * (j + 1) : 2], ident_f32[:])
            nc.scalar.copy(
                out=grouped_words[:, 2 * b : 2 * b + 2, :, :], in_=turned[:].rearrange("q (j u) p -> q j p u", u=2)
            )

        def matmul_mx(acc, stationary, tile_index, moving, start, stop):
            cols = slice(tile_index * P, (tile_index + 1) * P)
            nc.tensor.matmul_mx(
                out=acc[:],
                lhsT=stationary[0][:, cols].bitcast(E5M2),
                lhsT_scale=stationary[1][:, cols],
                rhs=moving[0][:].bitcast(E4M3),
                rhs_scale=moving[1][:],
                start=start,
                stop=stop,
            )

        def empty_bank(engine, out, acc):
            if engine == "vector":
                nc.vector.tensor_copy(out=out, in_=acc[:])
            else:
                nc.scalar.copy(out=out, in_=acc[:])

        dk_by_feature, dv_by_feature, dk_by_token = {}, {}, {}
        w_quant, x_quant = {}, {}
        out0_rows, out1_rows = {}, {}

        def out0_tile(g, j, c):
            if (g, j // 2) not in out0_rows:
                out0_rows[(g, j // 2)] = bigs.tile([P, 2, E], F32, name="st", tag="big")
            acc = ps_a.tile([P, N_TILE], F32, name="acc", tag="acc")
            matmul_mx(acc, dk_by_feature[g], j, w_quant[("k", c)], True, False)
            matmul_mx(acc, dv_by_feature[g], j, w_quant[("v", c)], False, True)
            empty_bank("scalar", out0_rows[(g, j // 2)][:, j % 2, c * N_TILE : (c + 1) * N_TILE], acc)

        def out0_store(g, b):
            nc.sync.dma_start(out=out0_hbm[g, b], in_=out0_rows[(g, b)][:])

        def out1_tile(m, c, engine):
            if m // 2 not in out1_rows:
                out1_rows[m // 2] = bigs.tile([P, 2, 2, E_HALF], F32, name="st", tag="big")
            acc = ps_a.tile([P, N_TILE], F32, name="acc", tag="acc")
            matmul_mx(acc, dk_by_token[0], m, x_quant[(0, c)], True, False)
            matmul_mx(acc, dk_by_token[1], m, x_quant[(1, c)], False, True)
            empty_bank(engine, out1_rows[m // 2][:, c // 2, m % 2, (c % 2) * N_TILE : (c % 2 + 1) * N_TILE], acc)

        def out1_store(a, h):
            nc.sync.dma_start(out=out1_hbm[a][:, :, h * E_HALF : (h + 1) * E_HALF], in_=out1_rows[a][:, h])

        def w_rows(w, c):
            return w_raw[w][:, c // 2, :, (c % 2) * N_TILE : (c % 2 + 1) * N_TILE]

        def x_rows(g, c):
            return x_raw[g][:, :, c * N_TILE : (c + 1) * N_TILE]

        def dz_rows(dz):
            return dz[:].rearrange("p (j w) -> p j w", j=PACK)

        dk0 = keep.tile([P, GROUPED], BF16, name="dk0")
        dv0 = keep.tile([P, GROUPED], BF16, name="dv0")
        dk0_turned = new_grouped()
        for b in range(2):
            cols = slice(b * HALF, (b + 1) * HALF)
            nc.vector.tensor_tensor(out=dk0[:, cols], in0=grad0[:, cols], in1=v0[:, cols], op=MULT)
            transpose_row_pair(dk0, dk0_turned, b)
        dk0_grouped = interleave_on_tensor(dz_rows(dk0))
        dv0_turned = new_grouped()
        for b in range(2):
            cols = slice(b * HALF, (b + 1) * HALF)
            nc.vector.tensor_tensor(out=dv0[:, cols], in0=grad0[:, cols], in1=k0[:, cols], op=MULT)
            transpose_row_pair(dv0, dv0_turned, b)
        dk_by_feature[0] = quantize(dk0_turned, E5M2, "dkt0")

        w_grouped = {}
        w_grouped[("k", 1)] = interleave_on_tensor(w_rows("k", 1))
        w_grouped[("k", 0)] = interleave_on_vector(w_rows("k", 0))
        dk_by_token[0] = quantize(dk0_grouped, E5M2, "dki0")
        dv_by_feature[0] = quantize(dv0_turned, E5M2, "dvt0")
        for h in range(2):
            w_grouped[("v", 2 * h + 1)] = interleave_on_tensor(w_rows("v", 2 * h + 1))
            w_grouped[("v", 2 * h)] = interleave_on_vector(w_rows("v", 2 * h))
            for c in (2 * h, 2 * h + 1):
                w_quant[("k", c)] = quantize(w_grouped[("k", c)], E4M3, "wk%d" % c)
            if h == 0:
                w_grouped[("k", 3)] = interleave_on_tensor(w_rows("k", 3))
                w_grouped[("k", 2)] = interleave_on_vector(w_rows("k", 2))
            for c in (2 * h, 2 * h + 1):
                w_quant[("v", c)] = quantize(w_grouped[("v", c)], E4M3, "wv%d" % c)

        for j in range(PACK):
            for c in (0, 1):
                out0_tile(0, j, c)

        dk1 = keep.tile([P, GROUPED], BF16, name="dk1")
        dv1 = keep.tile([P, GROUPED], BF16, name="dv1")
        nc.vector.tensor_tensor(out=dk1[:], in0=grad1[:], in1=vk1[:, 0, :], op=MULT)
        dk1_turned = new_grouped()
        transpose_row_pair(dk1, dk1_turned, 0)
        transpose_row_pair(dk1, dk1_turned, 1)
        for j in (0, 1):
            for c in (2, 3):
                out0_tile(0, j, c)
        out0_store(0, 0)
        nc.vector.tensor_tensor(out=dv1[:], in0=grad1[:], in1=vk1[:, 1, :], op=MULT)
        dv1_turned = new_grouped()
        transpose_row_pair(dv1, dv1_turned, 0)
        transpose_row_pair(dv1, dv1_turned, 1)
        for j in (2, 3):
            for c in (2, 3):
                out0_tile(0, j, c)
        out0_store(0, 1)

        def out0_pass1_then_out1_chunks_0_1():
            for j in range(PACK):
                for c in range(CHUNKS):
                    out0_tile(1, j, c)
                if j % 2 == 1:
                    out0_store(1, j // 2)
            for m in range(FEATURE_TILES):
                for c in (0, 1):
                    out1_tile(m, c, "scalar")
                if m % 2 == 1:
                    out1_store(m // 2, 0)

        def out1_chunk_2():
            for m in range(FEATURE_TILES):
                out1_tile(m, 2, "scalar")

        dk_by_feature[1] = quantize(dk1_turned, E5M2, "dkt1")
        jobs = [(0, 0), (0, 1), "dk1", (1, 0), (1, 1), (0, 2), (1, 2), (0, 3), (1, 3)]
        grouped_of = {}
        for n in range(len(jobs) + 1):
            if n < len(jobs):
                job = jobs[n]
                grouped_of[job] = interleave_on_vector(dz_rows(dk1) if job == "dk1" else x_rows(job[0], job[1]))
            if n == 1:
                dv_by_feature[1] = quantize(dv1_turned, E5M2, "dvt1")
            if n >= 1:
                job = jobs[n - 1]
                if job == "dk1":
                    dk_by_token[1] = quantize(grouped_of[job], E5M2, "dki1")
                else:
                    x_quant[job] = quantize(grouped_of[job], E4M3, "x%d_%d" % job)
                if job == (1, 1):
                    out0_pass1_then_out1_chunks_0_1()
                if job == (1, 2):
                    out1_chunk_2()

        for m in range(FEATURE_TILES):
            out1_tile(m, 3, "vector" if m % 2 == 0 else "scalar")
            if m % 2 == 1:
                out1_store(m // 2, 1)
